import numpy as np
import ml_dtypes


def mxq(x, axis, fmt="e4m3"):
    dtype, down = {"e4m3": (ml_dtypes.float8_e4m3fn, 7), "e5m2": (ml_dtypes.float8_e5m2, 14)}[fmt]
    v = np.moveaxis(np.asarray(x, np.float32).astype(ml_dtypes.bfloat16).astype(np.float64), axis, -1)
    blocks = v.reshape(v.shape[:-1] + (-1, 32))
    amax = np.abs(blocks).max(-1, keepdims=True)
    byte = np.maximum(np.where(amax > 0, np.frexp(amax)[1] - 1 + 127, 0) - down, 1)
    scale = np.exp2(byte - 127.0)
    codes = (blocks / scale).astype(np.float32).astype(dtype).astype(np.float64)
    return np.moveaxis((codes * scale).reshape(v.shape), -1, axis)


WIDE = False


def mx_kscale(k):
    if not WIDE:
        return np.ones(k)
    levels = np.array([10, -10, 5, -5, 0])
    if k % 512:
        return np.exp2(np.random.permutation(np.resize(levels, k // 32))).repeat(32)
    a = np.empty((k // 512, 16))
    for p in range(k // 512):
        a[p, :8] = np.random.permutation(np.resize(levels, 8))
        for g in range(8):
            far = levels[np.abs(levels - a[p, g]) >= 10]
            a[p, g + 8] = far[np.random.randint(len(far))]
    return np.exp2(a.ravel()).repeat(32)


BF16 = ml_dtypes.bfloat16


def bf(x):
    return np.asarray(x, np.float32).astype(BF16)


def f64(x):
    return np.asarray(x).astype(np.float64)


B, D_IN, D_FEAT, N_EX, N_LAB = 1024, 512, 512, 8192, 128
EPS = 1e-12


def l2_normalize(x):
    n = np.sqrt((x * x).sum(-1, keepdims=True))
    return x / np.maximum(n, EPS)


def draw0():
    s = mx_kscale(D_IN)
    return {"features": bf(np.random.standard_normal((B, D_IN)) * s),
            "ex_features": bf(np.random.standard_normal((N_EX, D_IN)) * s),
            "g_weight": bf(np.random.standard_normal((D_FEAT, D_IN)) / np.sqrt(D_IN) / s)}


def core(features, ex_features, g_weight):
    gq = mxq(f64(g_weight), 1, "e4m3")
    f = mxq(f64(features), 1, "e4m3") @ gq.T
    e = mxq(f64(ex_features), 1, "e4m3") @ gq.T
    return l2_normalize(f), l2_normalize(e)


def e4m3fn_bytes(y):
    return np.clip(np.asarray(y, np.float64), -448.0, 448.0).astype(np.float32).astype(ml_dtypes.float8_e4m3fn).view(np.uint8)


def e4m3fn_values(b):
    return np.asarray(b, np.uint8).view(ml_dtypes.float8_e4m3fn).astype(np.float64)


def setup_inputs():
    d = draw0()
    x0 = np.asarray(d['ex_features']).astype(np.float64)
    s = (np.max(np.abs(x0), axis=(0,), keepdims=True) / 448.0).astype(np.float32)
    out = {}
    for k, v in d.items():
        if k == 'ex_features':
            out['ex_features_bytes'] = e4m3fn_bytes(x0 / s.astype(np.float64))
            out['ex_features_scale'] = s
        else:
            out[k] = v
    return out


def reference(features, ex_features_bytes, ex_features_scale, g_weight):
    return core(features, e4m3fn_values(ex_features_bytes) * ex_features_scale.astype(np.float64), g_weight)

@@ -1,0 +1,239 @@
+from contextlib import ExitStack
+
+import concourse.mybir as mybir
+from concourse.masks import make_identity
+
+F32 = mybir.dt.float32
+BF16 = mybir.dt.bfloat16
+U32 = mybir.dt.uint32
+U8 = mybir.dt.uint8
+FP8 = mybir.dt.float8_e4m3fn
+FP8X4 = mybir.dt.float8_e4m3fn_x4
+ACT = mybir.ActivationFunctionType
+ALU = mybir.AluOpType
+
+P = 128
+K = 512
+N = 512
+B_ROWS = 1024
+E_ROWS = 8192
+EPS = 1e-12
+FLOPS = 2 * (B_ROWS + E_ROWS) * K * N
+
+PW = 2 * K
+G_PAIRS = N // (2 * P)
+F_PAIRS = B_ROWS // (2 * P)
+E_PAIRS = E_ROWS // (2 * P)
+FIRST_F = G_PAIRS
+FIRST_E = G_PAIRS + F_PAIRS
+LAST = G_PAIRS + F_PAIRS + E_PAIRS - 1
+CHUNK = 4
+
+WIDEN_AHEAD = 7
+S_NUM = 2
+S_DEN = 3
+FILL = False
+
+
+def tile_minerva_pb_kernel(tc, features, ex_features_bytes, ex_features_scale, g_weight, out_0, out_1):
+    nc = tc.nc
+
+    g_view = g_weight.rearrange("(j p) k -> p j k", p=P)
+    f_view = features.rearrange("(p j) k -> p (j k)", p=P)
+    b_view = ex_features_bytes.rearrange("(p j) k -> p (j k)", p=P)
+    o0_view = out_0.rearrange("(p j) n -> p (j n)", p=P)
+    o1_view = out_1.rearrange("(p j) n -> p (j n)", p=P)
+
+    with ExitStack() as ctx:
+        keep = ctx.enter_context(tc.tile_pool(name="keep", bufs=1))
+        work = ctx.enter_context(tc.tile_pool(name="work", bufs=4))
+        ahead = ctx.enter_context(tc.tile_pool(name="ahead", bufs=6))
+        small = ctx.enter_context(tc.tile_pool(name="small", bufs=6))
+        outs = ctx.enter_context(tc.tile_pool(name="outs", bufs=F_PAIRS + E_PAIRS))
+        psum_t = ctx.enter_context(tc.psum_pool(name="psum_t", bufs=2))
+        psum_a = ctx.enter_context(tc.psum_pool(name="psum_a", bufs=6))
+
+        ident = keep.tile([P, P], F32, name="ident")
+        make_identity(nc, ident[:])
+        one = keep.tile([P, 1], F32, name="one")
+        nc.vector.memset(one[:], 1.0)
+        one_root = keep.tile([P, 1], F32, name="one_root")
+        nc.scalar.activation(out=one_root[:], in_=one[:], func=ACT.Abs_reciprocal_sqrt)
+
+        plain = {}
+
+        def load_plain(m):
+            t = keep.tile([P, PW], BF16, name="plain%d" % m)
+            if m < FIRST_F:
+                nc.sync.dma_start(out=t[:].rearrange("p (j k) -> p j k", j=2), in_=g_view[:, 2 * m : 2 * m + 2, :])
+            else:
+                c0 = (m - FIRST_F) * PW
+                nc.sync.dma_start(out=t[:], in_=f_view[:, c0 : c0 + PW])
+            plain[m] = t
+
+        ex_bytes_sb = []
+
+        def load_bytes(c):
+            t = keep.tile([P, CHUNK * PW], U8, name="ex_bytes_sb%d" % c)
+            nc.sync.dma_start(out=t[:], in_=b_view[:, c * CHUNK * PW : (c + 1) * CHUNK * PW])
+            ex_bytes_sb.append(t)
+
+        scale2 = keep.tile([P, PW], F32, name="scale2")
+        for m in range(4):
+            load_plain(m)
+        nc.sync.dma_start(out=scale2[:, 0:K], in_=ex_features_scale.rearrange("o k -> (o k)").partition_broadcast(P))
+        load_bytes(0)
+        load_plain(4)
+        load_plain(5)
+        for c in range(1, E_PAIRS // CHUNK):
+            load_bytes(c)
+
+        g_codes = keep.tile([P, N], U32, name="g_codes", align_bytes=64)
+        g_scl = keep.tile([P, N], U8, name="g_scl", align_bytes=64)
+
+        xb = {}
+        tp = {}
+        grp = {}
+        codes = {}
+        scl = {}
+        acc = {}
+        ss = {}
+        cl = {}
+        rinv = {}
+        o = {}
+
+        def widen(m):
+            if m < FIRST_E or m > LAST:
+                return
+            q = m - FIRST_E
+            if q == 0:
+                nc.vector.tensor_copy(out=scale2[:, K : 2 * K], in_=scale2[:, 0:K])
+            xb[m] = ahead.tile([P, PW], BF16, name="xb", tag="xb")
+            c0 = (q % CHUNK) * PW
+            nc.vector.tensor_tensor(
+                out=xb[m][:],
+                in0=ex_bytes_sb[q // CHUNK][:, c0 : c0 + PW].bitcast(FP8),
+                in1=scale2[:],
+                op=ALU.mult,
+            )
+
+        def trans(m):
+            if m < 0 or m > LAST:
+                return
+            src = plain[m] if m < FIRST_E else xb[m]
+            tp[m] = psum_t.tile([P, 2, 2 * P], F32, name="tp", tag="tp")
+            if FILL and m > FIRST_F + 4:
+                nc.tensor.matmul_mx(
+                    out=tp[m][:].rearrange("p w c -> p (w c)"),
+                    lhsT=g_codes[:, 0:P].bitcast(FP8X4),
+                    lhsT_scale=g_scl[:, 0:P],
+                    rhs=g_codes[:].bitcast(FP8X4),
+                    rhs_scale=g_scl[:],
+                    start=True,
+                    stop=True,
+                )
+            for jj in range(2):
+                words = src[:, jj * K : (jj + 1) * K].bitcast(F32)
+                for w in range(2):
+                    nc.tensor.transpose(tp[m][:, w, jj * P : (jj + 1) * P], words[:, w : K // 2 : 2], ident[:])
+
+        def copyout(m, on_vector):
+            if m < 0 or m > LAST:
+                return
+            grp[m] = work.tile([P, PW], BF16, name="grp", tag="grp", align_bytes=64)
+            dst = grp[m][:].bitcast(F32).rearrange("p (c w) -> p c w", w=2)
+            if on_vector:
+                nc.vector.tensor_copy(out=dst, in_=tp[m][:].rearrange("p w c -> p c w"))
+            else:
+                nc.scalar.copy(out=dst, in_=tp[m][:].rearrange("p w c -> p c w"))
+
+        def quant(m):
+            if m < 0 or m > LAST:
+                return
+            if m < FIRST_F:
+                codes[m] = g_codes[:, m * 2 * P : (m + 1) * 2 * P]
+                scl[m] = g_scl[:, m * 2 * P : (m + 1) * 2 * P]
+            else:
+                c_t = work.tile([P, 2 * P], U32, name="codes", tag="codes", align_bytes=64)
+                s_t = work.tile([P, 2 * P], U8, name="scl", tag="scl", align_bytes=64)
+                codes[m] = c_t[:]
+                scl[m] = s_t[:]
+            nc.vector.quantize_mx(out=codes[m].bitcast(FP8X4), scales=scl[m], in_=grp[m][:])
+
+        def mm(m, j):
+            if m < FIRST_F or m > LAST:
+                return
+            acc[(m, j)] = psum_a.tile([P, N], F32, name="acc", tag="acc")
+            nc.tensor.matmul_mx(
+                out=acc[(m, j)][:],
+                lhsT=codes[m][:, j * P : (j + 1) * P].bitcast(FP8X4),
+                lhsT_scale=scl[m][:, j * P : (j + 1) * P],
+                rhs=g_codes[:].bitcast(FP8X4),
+                rhs_scale=g_scl[:],
+                start=True,
+                stop=True,
+            )
+
+        def sq(m, j):
+            if m < FIRST_F or m > LAST:
+                return
+            if j == 0:
+                ss[m] = small.tile([P, 2], F32, name="ss", tag="ss")
+            junk = work.tile([P, N], BF16, name="junk", tag="junk")
+            nc.scalar.activation(out=junk[:], in_=acc[(m, j)][:], func=ACT.Square, accum_out=ss[m][:, j : j + 1])
+
+        def over(m):
+            if m < FIRST_F or m > LAST:
+                return
+            cl[m] = small.tile([P, 2], F32, name="cl", tag="cl")
+            nc.scalar.activation(out=cl[m][:], in_=ss[m][:], func=ACT.Relu, bias=-EPS * EPS)
+
+        def rsqrt(m):
+            if m < FIRST_F or m > LAST:
+                return
+            rinv[m] = small.tile([P, 2], F32, name="rinv", tag="rinv")
+            nc.scalar.activation(out=rinv[m][:], in_=cl[m][:], func=ACT.Abs_reciprocal_sqrt, bias=EPS * EPS)
+
+        def scale_out(m, j, on_vector):
+            if m < FIRST_F or m > LAST:
+                return
+            if j == 0:
+                o[m] = outs.tile([P, 2 * N], F32, name="o", tag="o")
+            dst = o[m][:, j * N : (j + 1) * N]
+            if on_vector:
+                nc.vector.tensor_scalar(out=dst, in0=acc[(m, j)][:], scalar1=rinv[m][:, j : j + 1], scalar2=None, op0=ALU.mult)
+            else:
+                nc.scalar.activation(out=dst, in_=acc[(m, j)][:], func=ACT.Copy, scale=rinv[m][:, j : j + 1])
+
+        def store(m, j0, j1):
+            if m < FIRST_F or m > LAST:
+                return
+            if m < FIRST_E:
+                c0 = (m - FIRST_F) * 2 * N
+                dst = o0_view[:, c0 + j0 * N : c0 + j1 * N]
+            else:
+                c0 = (m - FIRST_E) * 2 * N
+                dst = o1_view[:, c0 + j0 * N : c0 + j1 * N]
+            nc.sync.dma_start(out=dst, in_=o[m][:, j0 * N : j1 * N])
+
+        with tc.manual_schedule():
+            for m in range(-4, LAST + 2):
+                late = m + WIDEN_AHEAD > LAST
+                sq(m, 0)
+                rsqrt(m - 1)
+                sq(m, 1)
+                trans(m + 4)
+                copyout(m + 3, m + 3 < FIRST_F or (late and m % 2 == 0))
+                over(m)
+                quant(m + 2)
+                on_scalar = ((m * S_NUM) % S_DEN < S_NUM and not late) or m - 1 == LAST
+                scale_out(m - 1, 0, True)
+                scale_out(m - 1, 1, not on_scalar)
+                mm(m + 2, 0)
+                mm(m + 2, 1)
+                widen(m + WIDEN_AHEAD)
+                if m - 1 == LAST:
+                    store(m - 1, 0, 1)
+                    store(m - 1, 1, 2)
+                else:
+                    store(m - 1, 0, 2)

@@ -79,9 +79,10 @@ def tile_minerva_pb_kernel(tc, features, ex_features_bytes, ex_features_scale, g
             ex_bytes_sb.append(t)
 
         scale2 = keep.tile([P, PW], F32, name="scale2")
+        sc_col = keep.tile([P, 4], F32, name="sc_col")
+        nc.sync.dma_start(out=sc_col[:], in_=ex_features_scale.rearrange("o (p t) -> p (o t)", p=P))
         for m in range(4):
             load_plain(m)
-        nc.sync.dma_start(out=scale2[:, 0:K], in_=ex_features_scale.rearrange("o k -> (o k)").partition_broadcast(P))
         load_bytes(0)
         load_plain(4)
         load_plain(5)
@@ -217,6 +218,10 @@ def tile_minerva_pb_kernel(tc, features, ex_features_bytes, ex_features_scale, g
             nc.sync.dma_start(out=dst, in_=o[m][:, j0 * N : j1 * N])
 
         with tc.manual_schedule():
+            sc_ps = psum_t.tile([P, 4, P], F32, name="sc_ps", tag="tp")
+            for t in range(4):
+                nc.tensor.transpose(sc_ps[:, t, :], sc_col[:, t : t + 1].to_broadcast([P, P]), ident[:])
+            nc.scalar.copy(out=scale2[:, 0:K].rearrange("p (c t) -> p c t", t=4), in_=sc_ps[:].rearrange("p t c -> p c t"))
             for m in range(-4, LAST + 2):
                 late = m + WIDEN_AHEAD > LAST
                 sq(m, 0)

@@ -27,7 +27,7 @@ E_PAIRS = E_ROWS // (2 * P)
 FIRST_F = G_PAIRS
 FIRST_E = G_PAIRS + F_PAIRS
 LAST = G_PAIRS + F_PAIRS + E_PAIRS - 1
-CHUNK = 4
+CHUNKS = [2, 2] + [4] * 7
 
 WIDEN_AHEAD = 7
 S_NUM = 2
@@ -71,22 +71,27 @@ def tile_minerva_pb_kernel(tc, features, ex_features_bytes, ex_features_scale, g
                 nc.sync.dma_start(out=t[:], in_=f_view[:, c0 : c0 + PW])
             plain[m] = t
 
-        ex_bytes_sb = []
+        ex_bytes_sb = {}
 
         def load_bytes(c):
-            t = keep.tile([P, CHUNK * PW], U8, name="ex_bytes_sb%d" % c)
-            nc.sync.dma_start(out=t[:], in_=b_view[:, c * CHUNK * PW : (c + 1) * CHUNK * PW])
-            ex_bytes_sb.append(t)
+            q0 = sum(CHUNKS[:c])
+            t = keep.tile([P, CHUNKS[c] * PW], U8, name="ex_bytes_sb%d" % c)
+            nc.sync.dma_start(out=t[:], in_=b_view[:, q0 * PW : (q0 + CHUNKS[c]) * PW])
+            for i in range(CHUNKS[c]):
+                ex_bytes_sb[q0 + i] = t[:, i * PW : (i + 1) * PW]
 
         scale2 = keep.tile([P, PW], F32, name="scale2")
         sc_col = keep.tile([P, 4], F32, name="sc_col")
         nc.sync.dma_start(out=sc_col[:], in_=ex_features_scale.rearrange("o (p t) -> p (o t)", p=P))
-        for m in range(4):
-            load_plain(m)
+        load_plain(0)
+        load_plain(1)
         load_bytes(0)
+        load_plain(2)
+        load_plain(3)
+        load_bytes(1)
         load_plain(4)
         load_plain(5)
-        for c in range(1, E_PAIRS // CHUNK):
+        for c in range(2, len(CHUNKS)):
             load_bytes(c)
 
         g_codes = keep.tile([P, N], U32, name="g_codes", align_bytes=64)
@@ -104,16 +109,15 @@ def tile_minerva_pb_kernel(tc, features, ex_features_bytes, ex_features_scale, g
         o = {}
 
         def widen(m):
-            if m < FIRST_E or m > LAST:
+            if m < FIRST_E or m > LAST or m in xb:
                 return
             q = m - FIRST_E
             if q == 0:
                 nc.vector.tensor_copy(out=scale2[:, K : 2 * K], in_=scale2[:, 0:K])
             xb[m] = ahead.tile([P, PW], BF16, name="xb", tag="xb")
-            c0 = (q % CHUNK) * PW
             nc.vector.tensor_tensor(
                 out=xb[m][:],
-                in0=ex_bytes_sb[q // CHUNK][:, c0 : c0 + PW].bitcast(FP8),
+                in0=ex_bytes_sb[q].bitcast(FP8),
                 in1=scale2[:],
                 op=ALU.mult,
             )
@@ -222,13 +226,14 @@ def tile_minerva_pb_kernel(tc, features, ex_features_bytes, ex_features_scale, g
             for t in range(4):
                 nc.tensor.transpose(sc_ps[:, t, :], sc_col[:, t : t + 1].to_broadcast([P, P]), ident[:])
             nc.scalar.copy(out=scale2[:, 0:K].rearrange("p (c t) -> p c t", t=4), in_=sc_ps[:].rearrange("p t c -> p c t"))
+            widen(FIRST_E)
             for m in range(-4, LAST + 2):
                 late = m + WIDEN_AHEAD > LAST
                 sq(m, 0)
                 rsqrt(m - 1)
                 sq(m, 1)
                 trans(m + 4)
-                copyout(m + 3, m + 3 < FIRST_F or (late and m % 2 == 0))
+                copyout(m + 3, late and m % 2 == 0)
                 over(m)
                 quant(m + 2)
                 on_scalar = ((m * S_NUM) % S_DEN < S_NUM and not late) or m - 1 == LAST

@@ -33,6 +33,7 @@ WIDEN_AHEAD = 7
 S_NUM = 2
 S_DEN = 3
 FILL = False
+FINE_STORES = 5
 
 
 def tile_minerva_pb_kernel(tc, features, ex_features_bytes, ex_features_scale, g_weight, out_0, out_1):
@@ -243,6 +244,9 @@ def tile_minerva_pb_kernel(tc, features, ex_features_bytes, ex_features_scale, g
                 mm(m + 2, 1)
                 widen(m + WIDEN_AHEAD)
                 if m - 1 == LAST:
+                    store(m - 1, 1, 2)
+                    store(m - 1, 0, 1)
+                elif m - 1 >= LAST - FINE_STORES:
                     store(m - 1, 0, 1)
                     store(m - 1, 1, 2)
                 else:

@@ -34,6 +34,8 @@ S_NUM = 2
 S_DEN = 3
 FILL = False
 FINE_STORES = 5
+WARM_FIRST = 7
+WARM_LAST = 5
 
 
 def tile_minerva_pb_kernel(tc, features, ex_features_bytes, ex_features_scale, g_weight, out_0, out_1):
@@ -60,6 +62,9 @@ def tile_minerva_pb_kernel(tc, features, ex_features_bytes, ex_features_scale, g
         nc.vector.memset(one[:], 1.0)
         one_root = keep.tile([P, 1], F32, name="one_root")
         nc.scalar.activation(out=one_root[:], in_=one[:], func=ACT.Abs_reciprocal_sqrt)
+
+        zeros = keep.tile([P, N], BF16, name="zeros")
+        nc.vector.memset(zeros[:], 0.0)
 
         plain = {}
 
@@ -142,6 +147,11 @@ def tile_minerva_pb_kernel(tc, features, ex_features_bytes, ex_features_scale, g
                 words = src[:, jj * K : (jj + 1) * K].bitcast(F32)
                 for w in range(2):
                     nc.tensor.transpose(tp[m][:, w, jj * P : (jj + 1) * P], words[:, w : K // 2 : 2], ident[:])
+            if m <= WARM_LAST:
+                dummy()
+
+        def dummy():
+            nc.tensor.matmul(out=idle_ps[:], lhsT=zeros[:, 0:P], rhs=zeros[:], start=True, stop=True)
 
         def copyout(m, on_vector):
             if m < 0 or m > LAST:
@@ -223,9 +233,13 @@ def tile_minerva_pb_kernel(tc, features, ex_features_bytes, ex_features_scale, g
             nc.sync.dma_start(out=dst, in_=o[m][:, j0 * N : j1 * N])
 
         with tc.manual_schedule():
+            idle_ps = psum_a.tile([P, N], F32, name="idle_ps", tag="acc")
+            for i in range(WARM_FIRST):
+                dummy()
             sc_ps = psum_t.tile([P, 4, P], F32, name="sc_ps", tag="tp")
             for t in range(4):
                 nc.tensor.transpose(sc_ps[:, t, :], sc_col[:, t : t + 1].to_broadcast([P, P]), ident[:])
+            dummy()
             nc.scalar.copy(out=scale2[:, 0:K].rearrange("p (c t) -> p c t", t=4), in_=sc_ps[:].rearrange("p t c -> p c t"))
             widen(FIRST_E)
             for m in range(-4, LAST + 2):

@@ -34,7 +34,7 @@ S_NUM = 2
 S_DEN = 3
 FILL = False
 FINE_STORES = 5
-WARM_FIRST = 7
+WARM_FIRST = 3
 WARM_LAST = 5
 
 

@@ -29,10 +29,7 @@ FIRST_E = G_PAIRS + F_PAIRS
 LAST = G_PAIRS + F_PAIRS + E_PAIRS - 1
 CHUNKS = [2, 2] + [4] * 7
 
-WIDEN_AHEAD = 7
-S_NUM = 2
-S_DEN = 3
-FILL = False
+CAST_AHEAD = 7
 FINE_STORES = 5
 WARM_FIRST = 3
 WARM_LAST = 5
@@ -86,7 +83,6 @@ def tile_minerva_pb_kernel(tc, features, ex_features_bytes, ex_features_scale, g
             for i in range(CHUNKS[c]):
                 ex_bytes_sb[q0 + i] = t[:, i * PW : (i + 1) * PW]
 
-        scale2 = keep.tile([P, PW], F32, name="scale2")
         sc_col = keep.tile([P, 4], F32, name="sc_col")
         nc.sync.dma_start(out=sc_col[:], in_=ex_features_scale.rearrange("o (p t) -> p (o t)", p=P))
         load_plain(0)
@@ -114,35 +110,17 @@ def tile_minerva_pb_kernel(tc, features, ex_features_bytes, ex_features_scale, g
         rinv = {}
         o = {}
 
-        def widen(m):
+        def cast(m):
             if m < FIRST_E or m > LAST or m in xb:
                 return
-            q = m - FIRST_E
-            if q == 0:
-                nc.vector.tensor_copy(out=scale2[:, K : 2 * K], in_=scale2[:, 0:K])
             xb[m] = ahead.tile([P, PW], BF16, name="xb", tag="xb")
-            nc.vector.tensor_tensor(
-                out=xb[m][:],
-                in0=ex_bytes_sb[q].bitcast(FP8),
-                in1=scale2[:],
-                op=ALU.mult,
-            )
+            nc.gpsimd.tensor_copy(out=xb[m][:], in_=ex_bytes_sb[m - FIRST_E].bitcast(FP8))
 
         def trans(m):
             if m < 0 or m > LAST:
                 return
             src = plain[m] if m < FIRST_E else xb[m]
             tp[m] = psum_t.tile([P, 2, 2 * P], F32, name="tp", tag="tp")
-            if FILL and m > FIRST_F + 4:
-                nc.tensor.matmul_mx(
-                    out=tp[m][:].rearrange("p w c -> p (w c)"),
-                    lhsT=g_codes[:, 0:P].bitcast(FP8X4),
-                    lhsT_scale=g_scl[:, 0:P],
-                    rhs=g_codes[:].bitcast(FP8X4),
-                    rhs_scale=g_scl[:],
-                    start=True,
-                    stop=True,
-                )
             for jj in range(2):
                 words = src[:, jj * K : (jj + 1) * K].bitcast(F32)
                 for w in range(2):
@@ -153,15 +131,20 @@ def tile_minerva_pb_kernel(tc, features, ex_features_bytes, ex_features_scale, g
         def dummy():
             nc.tensor.matmul(out=idle_ps[:], lhsT=zeros[:, 0:P], rhs=zeros[:], start=True, stop=True)
 
-        def copyout(m, on_vector):
+        def copyout(m):
             if m < 0 or m > LAST:
                 return
             grp[m] = work.tile([P, PW], BF16, name="grp", tag="grp", align_bytes=64)
+            if m >= FIRST_E:
+                nc.vector.tensor_tensor(
+                    out=grp[m][:].rearrange("p (c w h) -> p c w h", w=2, h=2),
+                    in0=tp[m][:].bitcast(BF16).rearrange("p w (c h) -> p c w h", h=2),
+                    in1=sc_col[:].rearrange("p (w h) -> p w h", w=2).unsqueeze(1).to_broadcast([P, 2 * P, 2, 2]),
+                    op=ALU.mult,
+                )
+                return
             dst = grp[m][:].bitcast(F32).rearrange("p (c w) -> p c w", w=2)
-            if on_vector:
-                nc.vector.tensor_copy(out=dst, in_=tp[m][:].rearrange("p w c -> p c w"))
-            else:
-                nc.scalar.copy(out=dst, in_=tp[m][:].rearrange("p w c -> p c w"))
+            nc.scalar.copy(out=dst, in_=tp[m][:].rearrange("p w c -> p c w"))
 
         def quant(m):
             if m < 0 or m > LAST:
@@ -236,27 +219,22 @@ def tile_minerva_pb_kernel(tc, features, ex_features_bytes, ex_features_scale, g
             idle_ps = psum_a.tile([P, N], F32, name="idle_ps", tag="acc")
             for i in range(WARM_FIRST):
                 dummy()
-            sc_ps = psum_t.tile([P, 4, P], F32, name="sc_ps", tag="tp")
-            for t in range(4):
-                nc.tensor.transpose(sc_ps[:, t, :], sc_col[:, t : t + 1].to_broadcast([P, P]), ident[:])
-            dummy()
-            nc.scalar.copy(out=scale2[:, 0:K].rearrange("p (c t) -> p c t", t=4), in_=sc_ps[:].rearrange("p t c -> p c t"))
-            widen(FIRST_E)
+            for m in range(FIRST_E, FIRST_E + 4):
+                cast(m)
             for m in range(-4, LAST + 2):
-                late = m + WIDEN_AHEAD > LAST
                 sq(m, 0)
                 rsqrt(m - 1)
                 sq(m, 1)
                 trans(m + 4)
-                copyout(m + 3, late and m % 2 == 0)
+                copyout(m + 3)
                 over(m)
                 quant(m + 2)
-                on_scalar = ((m * S_NUM) % S_DEN < S_NUM and not late) or m - 1 == LAST
+                on_scalar = (m - 1 >= FIRST_E and m + 3 <= LAST) or m - 1 == LAST
                 scale_out(m - 1, 0, True)
                 scale_out(m - 1, 1, not on_scalar)
                 mm(m + 2, 0)
                 mm(m + 2, 1)
-                widen(m + WIDEN_AHEAD)
+                cast(m + CAST_AHEAD)
                 if m - 1 == LAST:
                     store(m - 1, 1, 2)
                     store(m - 1, 0, 1)

@@ -29,7 +29,7 @@ FIRST_E = G_PAIRS + F_PAIRS
 LAST = G_PAIRS + F_PAIRS + E_PAIRS - 1
 CHUNKS = [2, 2] + [4] * 7
 
-CAST_AHEAD = 7
+RING = 4
 FINE_STORES = 5
 WARM_FIRST = 3
 WARM_LAST = 5
@@ -47,7 +47,7 @@ def tile_minerva_pb_kernel(tc, features, ex_features_bytes, ex_features_scale, g
     with ExitStack() as ctx:
         keep = ctx.enter_context(tc.tile_pool(name="keep", bufs=1))
         work = ctx.enter_context(tc.tile_pool(name="work", bufs=4))
-        ahead = ctx.enter_context(tc.tile_pool(name="ahead", bufs=6))
+        ring = ctx.enter_context(tc.tile_pool(name="ring", bufs=RING))
         small = ctx.enter_context(tc.tile_pool(name="small", bufs=6))
         outs = ctx.enter_context(tc.tile_pool(name="outs", bufs=F_PAIRS + E_PAIRS))
         psum_t = ctx.enter_context(tc.psum_pool(name="psum_t", bufs=2))
@@ -113,7 +113,7 @@ def tile_minerva_pb_kernel(tc, features, ex_features_bytes, ex_features_scale, g
         def cast(m):
             if m < FIRST_E or m > LAST or m in xb:
                 return
-            xb[m] = ahead.tile([P, PW], BF16, name="xb", tag="xb")
+            xb[m] = ring.tile([P, PW], BF16, name="xb", tag="xb", align_bytes=64)
             nc.gpsimd.tensor_copy(out=xb[m][:], in_=ex_bytes_sb[m - FIRST_E].bitcast(FP8))
 
         def trans(m):
@@ -134,8 +134,8 @@ def tile_minerva_pb_kernel(tc, features, ex_features_bytes, ex_features_scale, g
         def copyout(m):
             if m < 0 or m > LAST:
                 return
-            grp[m] = work.tile([P, PW], BF16, name="grp", tag="grp", align_bytes=64)
             if m >= FIRST_E:
+                grp[m] = xb[m]
                 nc.vector.tensor_tensor(
                     out=grp[m][:].rearrange("p (c w h) -> p c w h", w=2, h=2),
                     in0=tp[m][:].bitcast(BF16).rearrange("p w (c h) -> p c w h", h=2),
@@ -143,6 +143,7 @@ def tile_minerva_pb_kernel(tc, features, ex_features_bytes, ex_features_scale, g
                     op=ALU.mult,
                 )
                 return
+            grp[m] = work.tile([P, PW], BF16, name="grp", tag="grp", align_bytes=64)
             dst = grp[m][:].bitcast(F32).rearrange("p (c w) -> p c w", w=2)
             nc.scalar.copy(out=dst, in_=tp[m][:].rearrange("p w c -> p c w"))
 
@@ -219,7 +220,7 @@ def tile_minerva_pb_kernel(tc, features, ex_features_bytes, ex_features_scale, g
             idle_ps = psum_a.tile([P, N], F32, name="idle_ps", tag="acc")
             for i in range(WARM_FIRST):
                 dummy()
-            for m in range(FIRST_E, FIRST_E + 4):
+            for m in range(FIRST_E, FIRST_E + RING):
                 cast(m)
             for m in range(-4, LAST + 2):
                 sq(m, 0)
@@ -229,12 +230,13 @@ def tile_minerva_pb_kernel(tc, features, ex_features_bytes, ex_features_scale, g
                 copyout(m + 3)
                 over(m)
                 quant(m + 2)
+                if m + 2 >= FIRST_E:
+                    cast(m + 2 + RING)
                 on_scalar = (m - 1 >= FIRST_E and m + 3 <= LAST) or m - 1 == LAST
                 scale_out(m - 1, 0, True)
                 scale_out(m - 1, 1, not on_scalar)
                 mm(m + 2, 0)
                 mm(m + 2, 1)
-                cast(m + CAST_AHEAD)
                 if m - 1 == LAST:
                     store(m - 1, 1, 2)
                     store(m - 1, 0, 1)

@@ -24,11 +24,16 @@ PW = 2 * K
 G_PAIRS = N // (2 * P)
 F_PAIRS = B_ROWS // (2 * P)
 E_PAIRS = E_ROWS // (2 * P)
-FIRST_F = G_PAIRS
-FIRST_E = G_PAIRS + F_PAIRS
-LAST = G_PAIRS + F_PAIRS + E_PAIRS - 1
 CHUNKS = [2, 2] + [4] * 7
 
+F_FIRST = 1
+ORDER = (
+    [("g", q) for q in range(G_PAIRS)]
+    + [("f", q) for q in range(F_FIRST)]
+    + [("e", q) for q in range(E_PAIRS)]
+    + [("f", q) for q in range(F_FIRST, F_PAIRS)]
+)
+LAST = len(ORDER) - 1
 RING = 4
 FINE_STORES = 5
 WARM_FIRST = 3
@@ -65,14 +70,14 @@ def tile_minerva_pb_kernel(tc, features, ex_features_bytes, ex_features_scale, g
 
         plain = {}
 
-        def load_plain(m):
-            t = keep.tile([P, PW], BF16, name="plain%d" % m)
-            if m < FIRST_F:
-                nc.sync.dma_start(out=t[:].rearrange("p (j k) -> p j k", j=2), in_=g_view[:, 2 * m : 2 * m + 2, :])
+        def load_plain(i):
+            kind, q = ORDER[i]
+            t = keep.tile([P, PW], BF16, name="plain%d" % i)
+            if kind == "g":
+                nc.sync.dma_start(out=t[:].rearrange("p (j k) -> p j k", j=2), in_=g_view[:, 2 * q : 2 * q + 2, :])
             else:
-                c0 = (m - FIRST_F) * PW
-                nc.sync.dma_start(out=t[:], in_=f_view[:, c0 : c0 + PW])
-            plain[m] = t
+                nc.sync.dma_start(out=t[:], in_=f_view[:, q * PW : (q + 1) * PW])
+            plain[i] = t
 
         ex_bytes_sb = {}
 
@@ -85,16 +90,15 @@ def tile_minerva_pb_kernel(tc, features, ex_features_bytes, ex_features_scale, g
 
         sc_col = keep.tile([P, 4], F32, name="sc_col")
         nc.sync.dma_start(out=sc_col[:], in_=ex_features_scale.rearrange("o (p t) -> p (o t)", p=P))
-        load_plain(0)
-        load_plain(1)
+        for i in range(G_PAIRS):
+            load_plain(i)
         load_bytes(0)
-        load_plain(2)
-        load_plain(3)
-        load_bytes(1)
-        load_plain(4)
-        load_plain(5)
-        for c in range(2, len(CHUNKS)):
+        for i in range(G_PAIRS, G_PAIRS + F_FIRST):
+            load_plain(i)
+        for c in range(1, len(CHUNKS)):
             load_bytes(c)
+        for i in range(G_PAIRS + F_FIRST + E_PAIRS, LAST + 1):
+            load_plain(i)
 
         g_codes = keep.tile([P, N], U32, name="g_codes", align_bytes=64)
         g_scl = keep.tile([P, N], U8, name="g_scl", align_bytes=64)
@@ -109,139 +113,143 @@ def tile_minerva_pb_kernel(tc, features, ex_features_bytes, ex_features_scale, g
         cl = {}
         rinv = {}
         o = {}
+        ex_at = [i for i in range(LAST + 1) if ORDER[i][0] == "e"]
 
-        def cast(m):
-            if m < FIRST_E or m > LAST or m in xb:
-                return
-            xb[m] = ring.tile([P, PW], BF16, name="xb", tag="xb", align_bytes=64)
-            nc.gpsimd.tensor_copy(out=xb[m][:], in_=ex_bytes_sb[m - FIRST_E].bitcast(FP8))
+        def inside(i, kinds="gfe"):
+            return 0 <= i <= LAST and ORDER[i][0] in kinds
 
-        def trans(m):
-            if m < 0 or m > LAST:
+        def cast(n):
+            if n >= E_PAIRS:
                 return
-            src = plain[m] if m < FIRST_E else xb[m]
-            tp[m] = psum_t.tile([P, 2, 2 * P], F32, name="tp", tag="tp")
-            for jj in range(2):
-                words = src[:, jj * K : (jj + 1) * K].bitcast(F32)
-                for w in range(2):
-                    nc.tensor.transpose(tp[m][:, w, jj * P : (jj + 1) * P], words[:, w : K // 2 : 2], ident[:])
-            if m <= WARM_LAST:
-                dummy()
+            i = ex_at[n]
+            xb[i] = ring.tile([P, PW], BF16, name="xb", tag="xb", align_bytes=64)
+            nc.gpsimd.tensor_copy(out=xb[i][:], in_=ex_bytes_sb[n].bitcast(FP8))
 
         def dummy():
             nc.tensor.matmul(out=idle_ps[:], lhsT=zeros[:, 0:P], rhs=zeros[:], start=True, stop=True)
 
-        def copyout(m):
-            if m < 0 or m > LAST:
+        def trans(i):
+            if not inside(i):
                 return
-            if m >= FIRST_E:
-                grp[m] = xb[m]
+            src = xb[i] if ORDER[i][0] == "e" else plain[i]
+            tp[i] = psum_t.tile([P, 2, 2 * P], F32, name="tp", tag="tp")
+            for jj in range(2):
+                words = src[:, jj * K : (jj + 1) * K].bitcast(F32)
+                for w in range(2):
+                    nc.tensor.transpose(tp[i][:, w, jj * P : (jj + 1) * P], words[:, w : K // 2 : 2], ident[:])
+            if i <= WARM_LAST:
+                dummy()
+
+        def copyout(i):
+            if not inside(i):
+                return
+            if ORDER[i][0] == "e":
+                grp[i] = xb[i]
                 nc.vector.tensor_tensor(
-                    out=grp[m][:].rearrange("p (c w h) -> p c w h", w=2, h=2),
-                    in0=tp[m][:].bitcast(BF16).rearrange("p w (c h) -> p c w h", h=2),
+                    out=grp[i][:].rearrange("p (c w h) -> p c w h", w=2, h=2),
+                    in0=tp[i][:].bitcast(BF16).rearrange("p w (c h) -> p c w h", h=2),
                     in1=sc_col[:].rearrange("p (w h) -> p w h", w=2).unsqueeze(1).to_broadcast([P, 2 * P, 2, 2]),
                     op=ALU.mult,
                 )
                 return
-            grp[m] = work.tile([P, PW], BF16, name="grp", tag="grp", align_bytes=64)
-            dst = grp[m][:].bitcast(F32).rearrange("p (c w) -> p c w", w=2)
-            nc.scalar.copy(out=dst, in_=tp[m][:].rearrange("p w c -> p c w"))
+            grp[i] = work.tile([P, PW], BF16, name="grp", tag="grp", align_bytes=64)
+            dst = grp[i][:].bitcast(F32).rearrange("p (c w) -> p c w", w=2)
+            nc.scalar.copy(out=dst, in_=tp[i][:].rearrange("p w c -> p c w"))
 
-        def quant(m):
-            if m < 0 or m > LAST:
+        def quant(i):
+            if not inside(i):
                 return
-            if m < FIRST_F:
-                codes[m] = g_codes[:, m * 2 * P : (m + 1) * 2 * P]
-                scl[m] = g_scl[:, m * 2 * P : (m + 1) * 2 * P]
+            kind, q = ORDER[i]
+            if kind == "g":
+                codes[i] = g_codes[:, q * 2 * P : (q + 1) * 2 * P]
+                scl[i] = g_scl[:, q * 2 * P : (q + 1) * 2 * P]
             else:
                 c_t = work.tile([P, 2 * P], U32, name="codes", tag="codes", align_bytes=64)
                 s_t = work.tile([P, 2 * P], U8, name="scl", tag="scl", align_bytes=64)
-                codes[m] = c_t[:]
-                scl[m] = s_t[:]
-            nc.vector.quantize_mx(out=codes[m].bitcast(FP8X4), scales=scl[m], in_=grp[m][:])
+                codes[i] = c_t[:]
+                scl[i] = s_t[:]
+            nc.vector.quantize_mx(out=codes[i].bitcast(FP8X4), scales=scl[i], in_=grp[i][:])
+            if kind == "e":
+                cast(q + RING)
 
-        def mm(m, j):
-            if m < FIRST_F or m > LAST:
+        def mm(i, j):
+            if not inside(i, "fe"):
                 return
-            acc[(m, j)] = psum_a.tile([P, N], F32, name="acc", tag="acc")
+            acc[(i, j)] = psum_a.tile([P, N], F32, name="acc", tag="acc")
             nc.tensor.matmul_mx(
-                out=acc[(m, j)][:],
-                lhsT=codes[m][:, j * P : (j + 1) * P].bitcast(FP8X4),
-                lhsT_scale=scl[m][:, j * P : (j + 1) * P],
+                out=acc[(i, j)][:],
+                lhsT=codes[i][:, j * P : (j + 1) * P].bitcast(FP8X4),
+                lhsT_scale=scl[i][:, j * P : (j + 1) * P],
                 rhs=g_codes[:].bitcast(FP8X4),
                 rhs_scale=g_scl[:],
                 start=True,
                 stop=True,
             )
 
-        def sq(m, j):
-            if m < FIRST_F or m > LAST:
+        def sq(i, j):
+            if not inside(i, "fe"):
                 return
             if j == 0:
-                ss[m] = small.tile([P, 2], F32, name="ss", tag="ss")
+                ss[i] = small.tile([P, 2], F32, name="ss", tag="ss")
             junk = work.tile([P, N], BF16, name="junk", tag="junk")
-            nc.scalar.activation(out=junk[:], in_=acc[(m, j)][:], func=ACT.Square, accum_out=ss[m][:, j : j + 1])
+            nc.scalar.activation(out=junk[:], in_=acc[(i, j)][:], func=ACT.Square, accum_out=ss[i][:, j : j + 1])
 
-        def over(m):
-            if m < FIRST_F or m > LAST:
+        def over(i):
+            if not inside(i, "fe"):
                 return
-            cl[m] = small.tile([P, 2], F32, name="cl", tag="cl")
-            nc.scalar.activation(out=cl[m][:], in_=ss[m][:], func=ACT.Relu, bias=-EPS * EPS)
+            cl[i] = small.tile([P, 2], F32, name="cl", tag="cl")
+            nc.scalar.activation(out=cl[i][:], in_=ss[i][:], func=ACT.Relu, bias=-EPS * EPS)
 
-        def rsqrt(m):
-            if m < FIRST_F or m > LAST:
+        def rsqrt(i):
+            if not inside(i, "fe"):
                 return
-            rinv[m] = small.tile([P, 2], F32, name="rinv", tag="rinv")
-            nc.scalar.activation(out=rinv[m][:], in_=cl[m][:], func=ACT.Abs_reciprocal_sqrt, bias=EPS * EPS)
+            rinv[i] = small.tile([P, 2], F32, name="rinv", tag="rinv")
+            nc.scalar.activation(out=rinv[i][:], in_=cl[i][:], func=ACT.Abs_reciprocal_sqrt, bias=EPS * EPS)
 
-        def scale_out(m, j, on_vector):
-            if m < FIRST_F or m > LAST:
+        def scale_out(i, j, on_vector):
+            if not inside(i, "fe"):
                 return
-            if j == 0:
-                o[m] = outs.tile([P, 2 * N], F32, name="o", tag="o")
-            dst = o[m][:, j * N : (j + 1) * N]
+            if i not in o:
+                o[i] = outs.tile([P, 2 * N], F32, name="o", tag="o")
+            dst = o[i][:, j * N : (j + 1) * N]
             if on_vector:
-                nc.vector.tensor_scalar(out=dst, in0=acc[(m, j)][:], scalar1=rinv[m][:, j : j + 1], scalar2=None, op0=ALU.mult)
+                nc.vector.tensor_scalar(out=dst, in0=acc[(i, j)][:], scalar1=rinv[i][:, j : j + 1], scalar2=None, op0=ALU.mult)
             else:
-                nc.scalar.activation(out=dst, in_=acc[(m, j)][:], func=ACT.Copy, scale=rinv[m][:, j : j + 1])
+                nc.scalar.activation(out=dst, in_=acc[(i, j)][:], func=ACT.Copy, scale=rinv[i][:, j : j + 1])
 
-        def store(m, j0, j1):
-            if m < FIRST_F or m > LAST:
+        def store(i, j0, j1):
+            if not inside(i, "fe"):
                 return
-            if m < FIRST_E:
-                c0 = (m - FIRST_F) * 2 * N
-                dst = o0_view[:, c0 + j0 * N : c0 + j1 * N]
-            else:
-                c0 = (m - FIRST_E) * 2 * N
-                dst = o1_view[:, c0 + j0 * N : c0 + j1 * N]
-            nc.sync.dma_start(out=dst, in_=o[m][:, j0 * N : j1 * N])
+            kind, q = ORDER[i]
+            view = o0_view if kind == "f" else o1_view
+            c0 = q * 2 * N
+            nc.sync.dma_start(out=view[:, c0 + j0 * N : c0 + j1 * N], in_=o[i][:, j0 * N : j1 * N])
 
         with tc.manual_schedule():
             idle_ps = psum_a.tile([P, N], F32, name="idle_ps", tag="acc")
             for i in range(WARM_FIRST):
                 dummy()
-            for m in range(FIRST_E, FIRST_E + RING):
-                cast(m)
-            for m in range(-4, LAST + 2):
-                sq(m, 0)
-                rsqrt(m - 1)
-                sq(m, 1)
-                trans(m + 4)
-                copyout(m + 3)
-                over(m)
-                quant(m + 2)
-                if m + 2 >= FIRST_E:
-                    cast(m + 2 + RING)
-                on_scalar = (m - 1 >= FIRST_E and m + 3 <= LAST) or m - 1 == LAST
-                scale_out(m - 1, 0, True)
-                scale_out(m - 1, 1, not on_scalar)
-                mm(m + 2, 0)
-                mm(m + 2, 1)
-                if m - 1 == LAST:
-                    store(m - 1, 1, 2)
-                    store(m - 1, 0, 1)
-                elif m - 1 >= LAST - FINE_STORES:
-                    store(m - 1, 0, 1)
-                    store(m - 1, 1, 2)
+            for n in range(RING):
+                cast(n)
+            for s in range(-4, LAST + 2):
+                sq(s, 0)
+                rsqrt(s - 1)
+                sq(s, 1)
+                trans(s + 4)
+                copyout(s + 3)
+                over(s)
+                quant(s + 2)
+                both_vector = not inside(s + 3, "e") and s - 1 != LAST
+                both_scalar = s % 10 == 0 and not both_vector
+                scale_out(s - 1, 0, not both_scalar)
+                scale_out(s - 1, 1, both_vector)
+                mm(s + 2, 0)
+                mm(s + 2, 1)
+                if s - 1 == LAST:
+                    store(s - 1, 1, 2)
+                    store(s - 1, 0, 1)
+                elif s - 1 >= LAST - FINE_STORES:
+                    store(s - 1, 0, 1)
+                    store(s - 1, 1, 2)
                 else:
-                    store(m - 1, 0, 2)
+                    store(s - 1, 0, 2)

@@ -26,7 +26,7 @@ F_PAIRS = B_ROWS // (2 * P)
 E_PAIRS = E_ROWS // (2 * P)
 CHUNKS = [2, 2] + [4] * 7
 
-F_FIRST = 1
+F_FIRST = 2
 ORDER = (
     [("g", q) for q in range(G_PAIRS)]
     + [("f", q) for q in range(F_FIRST)]
@@ -34,7 +34,7 @@ ORDER = (
     + [("f", q) for q in range(F_FIRST, F_PAIRS)]
 )
 LAST = len(ORDER) - 1
-RING = 4
+RING = 3
 FINE_STORES = 5
 WARM_FIRST = 3
 WARM_LAST = 5
@@ -85,8 +85,8 @@ def tile_minerva_pb_kernel(tc, features, ex_features_bytes, ex_features_scale, g
             q0 = sum(CHUNKS[:c])
             t = keep.tile([P, CHUNKS[c] * PW], U8, name="ex_bytes_sb%d" % c)
             nc.sync.dma_start(out=t[:], in_=b_view[:, q0 * PW : (q0 + CHUNKS[c]) * PW])
-            for i in range(CHUNKS[c]):
-                ex_bytes_sb[q0 + i] = t[:, i * PW : (i + 1) * PW]
+            for i in range(0, CHUNKS[c], 2):
+                ex_bytes_sb[q0 + i] = t[:, i * PW : (i + 2) * PW]
 
         sc_col = keep.tile([P, 4], F32, name="sc_col")
         nc.sync.dma_start(out=sc_col[:], in_=ex_features_scale.rearrange("o (p t) -> p (o t)", p=P))
@@ -121,9 +121,10 @@ def tile_minerva_pb_kernel(tc, features, ex_features_bytes, ex_features_scale, g
         def cast(n):
             if n >= E_PAIRS:
                 return
-            i = ex_at[n]
-            xb[i] = ring.tile([P, PW], BF16, name="xb", tag="xb", align_bytes=64)
-            nc.gpsimd.tensor_copy(out=xb[i][:], in_=ex_bytes_sb[n].bitcast(FP8))
+            both = ring.tile([P, 2 * PW], BF16, name="xb", tag="xb", align_bytes=64)
+            nc.gpsimd.tensor_copy(out=both[:], in_=ex_bytes_sb[n].bitcast(FP8))
+            for h in range(2):
+                xb[ex_at[n + h]] = both[:, h * PW : (h + 1) * PW]
 
         def dummy():
             nc.tensor.matmul(out=idle_ps[:], lhsT=zeros[:, 0:P], rhs=zeros[:], start=True, stop=True)
@@ -146,14 +147,15 @@ def tile_minerva_pb_kernel(tc, features, ex_features_bytes, ex_features_scale, g
             if ORDER[i][0] == "e":
                 grp[i] = xb[i]
                 nc.vector.tensor_tensor(
-                    out=grp[i][:].rearrange("p (c w h) -> p c w h", w=2, h=2),
+                    out=grp[i].rearrange("p (c w h) -> p c w h", w=2, h=2),
                     in0=tp[i][:].bitcast(BF16).rearrange("p w (c h) -> p c w h", h=2),
                     in1=sc_col[:].rearrange("p (w h) -> p w h", w=2).unsqueeze(1).to_broadcast([P, 2 * P, 2, 2]),
                     op=ALU.mult,
                 )
                 return
-            grp[i] = work.tile([P, PW], BF16, name="grp", tag="grp", align_bytes=64)
-            dst = grp[i][:].bitcast(F32).rearrange("p (c w) -> p c w", w=2)
+            grp_t = work.tile([P, PW], BF16, name="grp", tag="grp", align_bytes=64)
+            grp[i] = grp_t[:]
+            dst = grp[i].bitcast(F32).rearrange("p (c w) -> p c w", w=2)
             nc.scalar.copy(out=dst, in_=tp[i][:].rearrange("p w c -> p c w"))
 
         def quant(i):
@@ -168,9 +170,9 @@ def tile_minerva_pb_kernel(tc, features, ex_features_bytes, ex_features_scale, g
                 s_t = work.tile([P, 2 * P], U8, name="scl", tag="scl", align_bytes=64)
                 codes[i] = c_t[:]
                 scl[i] = s_t[:]
-            nc.vector.quantize_mx(out=codes[i].bitcast(FP8X4), scales=scl[i], in_=grp[i][:])
-            if kind == "e":
-                cast(q + RING)
+            nc.vector.quantize_mx(out=codes[i].bitcast(FP8X4), scales=scl[i], in_=grp[i])
+            if kind == "e" and q % 2 == 1:
+                cast(q - 1 + 2 * RING)
 
         def mm(i, j):
             if not inside(i, "fe"):
@@ -230,26 +232,28 @@ def tile_minerva_pb_kernel(tc, features, ex_features_bytes, ex_features_scale, g
             for i in range(WARM_FIRST):
                 dummy()
             for n in range(RING):
-                cast(n)
-            for s in range(-4, LAST + 2):
-                sq(s, 0)
-                rsqrt(s - 1)
-                sq(s, 1)
-                trans(s + 4)
-                copyout(s + 3)
-                over(s)
+                cast(2 * n)
+            for s in range(-6, LAST + 2, 2):
                 quant(s + 2)
-                both_vector = not inside(s + 3, "e") and s - 1 != LAST
-                both_scalar = s % 10 == 0 and not both_vector
-                scale_out(s - 1, 0, not both_scalar)
-                scale_out(s - 1, 1, both_vector)
-                mm(s + 2, 0)
-                mm(s + 2, 1)
-                if s - 1 == LAST:
-                    store(s - 1, 1, 2)
-                    store(s - 1, 0, 1)
-                elif s - 1 >= LAST - FINE_STORES:
-                    store(s - 1, 0, 1)
-                    store(s - 1, 1, 2)
-                else:
-                    store(s - 1, 0, 2)
+                quant(s + 3)
+                for m in (s, s + 1):
+                    sq(m, 0)
+                    rsqrt(m - 1)
+                    sq(m, 1)
+                    over(m)
+                    both_vector = not inside(m + 4, "e") and m - 1 != LAST
+                    both_scalar = m % 10 == 0 and not both_vector
+                    scale_out(m - 1, 0, not both_scalar)
+                    scale_out(m - 1, 1, both_vector)
+                    mm(m + 2, 0)
+                    mm(m + 2, 1)
+                    copyout(m + 4)
+                    trans(m + 6)
+                    if m - 1 == LAST:
+                        store(m - 1, 1, 2)
+                        store(m - 1, 0, 1)
+                    elif m - 1 >= LAST - FINE_STORES:
+                        store(m - 1, 0, 1)
+                        store(m - 1, 1, 2)
+                    else:
+                        store(m - 1, 0, 2)

@@ -67,6 +67,8 @@ def tile_minerva_pb_kernel(tc, features, ex_features_bytes, ex_features_scale, g
 
         zeros = keep.tile([P, N], BF16, name="zeros")
         nc.vector.memset(zeros[:], 0.0)
+        first_copy = keep.tile([P, P], BF16, name="first_copy")
+        nc.gpsimd.tensor_copy(out=first_copy[:], in_=zeros[:, 0:P])
 
         plain = {}
 
@@ -122,9 +124,14 @@ def tile_minerva_pb_kernel(tc, features, ex_features_bytes, ex_features_scale, g
             if n >= E_PAIRS:
                 return
             both = ring.tile([P, 2 * PW], BF16, name="xb", tag="xb", align_bytes=64)
-            nc.gpsimd.tensor_copy(out=both[:], in_=ex_bytes_sb[n].bitcast(FP8))
             for h in range(2):
                 xb[ex_at[n + h]] = both[:, h * PW : (h + 1) * PW]
+            if n >= 2 * RING:
+                nc.gpsimd.tensor_copy(out=both[:], in_=ex_bytes_sb[n].bitcast(FP8))
+                return
+            for h in range(2):
+                cols = slice(h * PW, (h + 1) * PW)
+                nc.vector.tensor_copy(out=both[:, cols], in_=ex_bytes_sb[n][:, cols].bitcast(FP8))
 
         def dummy():
             nc.tensor.matmul(out=idle_ps[:], lhsT=zeros[:, 0:P], rhs=zeros[:], start=True, stop=True)
@@ -134,6 +141,16 @@ def tile_minerva_pb_kernel(tc, features, ex_features_bytes, ex_features_scale, g
                 return
             src = xb[i] if ORDER[i][0] == "e" else plain[i]
             tp[i] = psum_t.tile([P, 2, 2 * P], F32, name="tp", tag="tp")
+            if i > WARM_LAST:
+                nc.tensor.matmul_mx(
+                    out=tp[i][:].rearrange("p w c -> p (w c)"),
+                    lhsT=g_codes[:, 0:P].bitcast(FP8X4),
+                    lhsT_scale=g_scl[:, 0:P],
+                    rhs=g_codes[:].bitcast(FP8X4),
+                    rhs_scale=g_scl[:],
+                    start=True,
+                    stop=True,
+                )
             for jj in range(2):
                 words = src[:, jj * K : (jj + 1) * K].bitcast(F32)
                 for w in range(2):
@@ -231,19 +248,19 @@ def tile_minerva_pb_kernel(tc, features, ex_features_bytes, ex_features_scale, g
             idle_ps = psum_a.tile([P, N], F32, name="idle_ps", tag="acc")
             for i in range(WARM_FIRST):
                 dummy()
-            for n in range(RING):
-                cast(2 * n)
+            cast(0)
             for s in range(-6, LAST + 2, 2):
                 quant(s + 2)
                 quant(s + 3)
+                if -4 < s <= 0:
+                    cast(s + 4)
                 for m in (s, s + 1):
                     sq(m, 0)
                     rsqrt(m - 1)
                     sq(m, 1)
                     over(m)
                     both_vector = not inside(m + 4, "e") and m - 1 != LAST
-                    both_scalar = m % 10 == 0 and not both_vector
-                    scale_out(m - 1, 0, not both_scalar)
+                    scale_out(m - 1, 0, True)
                     scale_out(m - 1, 1, both_vector)
                     mm(m + 2, 0)
                     mm(m + 2, 1)

@@ -131,7 +131,10 @@ def tile_minerva_pb_kernel(tc, features, ex_features_bytes, ex_features_scale, g
                 return
             for h in range(2):
                 cols = slice(h * PW, (h + 1) * PW)
-                nc.vector.tensor_copy(out=both[:, cols], in_=ex_bytes_sb[n][:, cols].bitcast(FP8))
+                if n + h < RING:
+                    nc.vector.tensor_copy(out=both[:, cols], in_=ex_bytes_sb[n][:, cols].bitcast(FP8))
+                else:
+                    nc.scalar.copy(out=both[:, cols], in_=ex_bytes_sb[n][:, cols].bitcast(FP8))
 
         def dummy():
             nc.tensor.matmul(out=idle_ps[:], lhsT=zeros[:, 0:P], rhs=zeros[:], start=True, stop=True)

from contextlib import ExitStack

import concourse.mybir as mybir
from concourse.masks import make_identity

F32 = mybir.dt.float32
BF16 = mybir.dt.bfloat16
U32 = mybir.dt.uint32
U8 = mybir.dt.uint8
FP8 = mybir.dt.float8_e4m3fn
FP8X4 = mybir.dt.float8_e4m3fn_x4
ACT = mybir.ActivationFunctionType
ALU = mybir.AluOpType

P = 128
K = 512
N = 512
B_ROWS = 1024
E_ROWS = 8192
EPS = 1e-12
FLOPS = 2 * (B_ROWS + E_ROWS) * K * N

PW = 2 * K
G_PAIRS = N // (2 * P)
F_PAIRS = B_ROWS // (2 * P)
E_PAIRS = E_ROWS // (2 * P)
CHUNKS = [2, 2] + [4] * 7

F_FIRST = 2
ORDER = (
    [("g", q) for q in range(G_PAIRS)]
    + [("f", q) for q in range(F_FIRST)]
    + [("e", q) for q in range(E_PAIRS)]
    + [("f", q) for q in range(F_FIRST, F_PAIRS)]
)
LAST = len(ORDER) - 1
RING = 3
FINE_STORES = 5
WARM_FIRST = 3
WARM_LAST = 5


def tile_minerva_pb_kernel(tc, features, ex_features_bytes, ex_features_scale, g_weight, out_0, out_1):
    nc = tc.nc

    g_view = g_weight.rearrange("(j p) k -> p j k", p=P)
    f_view = features.rearrange("(p j) k -> p (j k)", p=P)
    b_view = ex_features_bytes.rearrange("(p j) k -> p (j k)", p=P)
    o0_view = out_0.rearrange("(p j) n -> p (j n)", p=P)
    o1_view = out_1.rearrange("(p j) n -> p (j n)", p=P)

    with ExitStack() as ctx:
        keep = ctx.enter_context(tc.tile_pool(name="keep", bufs=1))
        work = ctx.enter_context(tc.tile_pool(name="work", bufs=4))
        ring = ctx.enter_context(tc.tile_pool(name="ring", bufs=RING))
        small = ctx.enter_context(tc.tile_pool(name="small", bufs=6))
        outs = ctx.enter_context(tc.tile_pool(name="outs", bufs=F_PAIRS + E_PAIRS))
        psum_t = ctx.enter_context(tc.psum_pool(name="psum_t", bufs=2))
        psum_a = ctx.enter_context(tc.psum_pool(name="psum_a", bufs=6))

        ident = keep.tile([P, P], F32, name="ident")
        make_identity(nc, ident[:])
        one = keep.tile([P, 1], F32, name="one")
        nc.vector.memset(one[:], 1.0)
        one_root = keep.tile([P, 1], F32, name="one_root")
        nc.scalar.activation(out=one_root[:], in_=one[:], func=ACT.Abs_reciprocal_sqrt)

        zeros = keep.tile([P, N], BF16, name="zeros")
        nc.vector.memset(zeros[:], 0.0)
        first_copy = keep.tile([P, P], BF16, name="first_copy")
        nc.gpsimd.tensor_copy(out=first_copy[:], in_=zeros[:, 0:P])

        plain = {}

        def load_plain(i):
            kind, q = ORDER[i]
            t = keep.tile([P, PW], BF16, name="plain%d" % i)
            if kind == "g":
                nc.sync.dma_start(out=t[:].rearrange("p (j k) -> p j k", j=2), in_=g_view[:, 2 * q : 2 * q + 2, :])
            else:
                nc.sync.dma_start(out=t[:], in_=f_view[:, q * PW : (q + 1) * PW])
            plain[i] = t

        ex_bytes_sb = {}

        def load_bytes(c):
            q0 = sum(CHUNKS[:c])
            t = keep.tile([P, CHUNKS[c] * PW], U8, name="ex_bytes_sb%d" % c)
            nc.sync.dma_start(out=t[:], in_=b_view[:, q0 * PW : (q0 + CHUNKS[c]) * PW])
            for i in range(0, CHUNKS[c], 2):
                ex_bytes_sb[q0 + i] = t[:, i * PW : (i + 2) * PW]

        sc_col = keep.tile([P, 4], F32, name="sc_col")
        nc.sync.dma_start(out=sc_col[:], in_=ex_features_scale.rearrange("o (p t) -> p (o t)", p=P))
        for i in range(G_PAIRS):
            load_plain(i)
        load_bytes(0)
        for i in range(G_PAIRS, G_PAIRS + F_FIRST):
            load_plain(i)
        for c in range(1, len(CHUNKS)):
            load_bytes(c)
        for i in range(G_PAIRS + F_FIRST + E_PAIRS, LAST + 1):
            load_plain(i)

        g_codes = keep.tile([P, N], U32, name="g_codes", align_bytes=64)
        g_scl = keep.tile([P, N], U8, name="g_scl", align_bytes=64)

        xb = {}
        tp = {}
        grp = {}
        codes = {}
        scl = {}
        acc = {}
        ss = {}
        cl = {}
        rinv = {}
        o = {}
        ex_at = [i for i in range(LAST + 1) if ORDER[i][0] == "e"]

        def inside(i, kinds="gfe"):
            return 0 <= i <= LAST and ORDER[i][0] in kinds

        def cast(n):
            if n >= E_PAIRS:
                return
            both = ring.tile([P, 2 * PW], BF16, name="xb", tag="xb", align_bytes=64)
            for h in range(2):
                xb[ex_at[n + h]] = both[:, h * PW : (h + 1) * PW]
            if n >= 2 * RING:
                nc.gpsimd.tensor_copy(out=both[:], in_=ex_bytes_sb[n].bitcast(FP8))
                return
            for h in range(2):
                cols = slice(h * PW, (h + 1) * PW)
                if n + h < RING:
                    nc.vector.tensor_copy(out=both[:, cols], in_=ex_bytes_sb[n][:, cols].bitcast(FP8))
                else:
                    nc.scalar.copy(out=both[:, cols], in_=ex_bytes_sb[n][:, cols].bitcast(FP8))

        def dummy():
            nc.tensor.matmul(out=idle_ps[:], lhsT=zeros[:, 0:P], rhs=zeros[:], start=True, stop=True)

        def trans(i):
            if not inside(i):
                return
            src = xb[i] if ORDER[i][0] == "e" else plain[i]
            tp[i] = psum_t.tile([P, 2, 2 * P], F32, name="tp", tag="tp")
            if i > WARM_LAST:
                nc.tensor.matmul_mx(
                    out=tp[i][:].rearrange("p w c -> p (w c)"),
                    lhsT=g_codes[:, 0:P].bitcast(FP8X4),
                    lhsT_scale=g_scl[:, 0:P],
                    rhs=g_codes[:].bitcast(FP8X4),
                    rhs_scale=g_scl[:],
                    start=True,
                    stop=True,
                )
            for jj in range(2):
                words = src[:, jj * K : (jj + 1) * K].bitcast(F32)
                for w in range(2):
                    nc.tensor.transpose(tp[i][:, w, jj * P : (jj + 1) * P], words[:, w : K // 2 : 2], ident[:])
            if i <= WARM_LAST:
                dummy()

        def copyout(i):
            if not inside(i):
                return
            if ORDER[i][0] == "e":
                grp[i] = xb[i]
                nc.vector.tensor_tensor(
                    out=grp[i].rearrange("p (c w h) -> p c w h", w=2, h=2),
                    in0=tp[i][:].bitcast(BF16).rearrange("p w (c h) -> p c w h", h=2),
                    in1=sc_col[:].rearrange("p (w h) -> p w h", w=2).unsqueeze(1).to_broadcast([P, 2 * P, 2, 2]),
                    op=ALU.mult,
                )
                return
            grp_t = work.tile([P, PW], BF16, name="grp", tag="grp", align_bytes=64)
            grp[i] = grp_t[:]
            dst = grp[i].bitcast(F32).rearrange("p (c w) -> p c w", w=2)
            nc.scalar.copy(out=dst, in_=tp[i][:].rearrange("p w c -> p c w"))

        def quant(i):
            if not inside(i):
                return
            kind, q = ORDER[i]
            if kind == "g":
                codes[i] = g_codes[:, q * 2 * P : (q + 1) * 2 * P]
                scl[i] = g_scl[:, q * 2 * P : (q + 1) * 2 * P]
            else:
                c_t = work.tile([P, 2 * P], U32, name="codes", tag="codes", align_bytes=64)
                s_t = work.tile([P, 2 * P], U8, name="scl", tag="scl", align_bytes=64)
                codes[i] = c_t[:]
                scl[i] = s_t[:]
            nc.vector.quantize_mx(out=codes[i].bitcast(FP8X4), scales=scl[i], in_=grp[i])
            if kind == "e" and q % 2 == 1:
                cast(q - 1 + 2 * RING)

        def mm(i, j):
            if not inside(i, "fe"):
                return
            acc[(i, j)] = psum_a.tile([P, N], F32, name="acc", tag="acc")
            nc.tensor.matmul_mx(
                out=acc[(i, j)][:],
                lhsT=codes[i][:, j * P : (j + 1) * P].bitcast(FP8X4),
                lhsT_scale=scl[i][:, j * P : (j + 1) * P],
                rhs=g_codes[:].bitcast(FP8X4),
                rhs_scale=g_scl[:],
                start=True,
                stop=True,
            )

        def sq(i, j):
            if not inside(i, "fe"):
                return
            if j == 0:
                ss[i] = small.tile([P, 2], F32, name="ss", tag="ss")
            junk = work.tile([P, N], BF16, name="junk", tag="junk")
            nc.scalar.activation(out=junk[:], in_=acc[(i, j)][:], func=ACT.Square, accum_out=ss[i][:, j : j + 1])

        def over(i):
            if not inside(i, "fe"):
                return
            cl[i] = small.tile([P, 2], F32, name="cl", tag="cl")
            nc.scalar.activation(out=cl[i][:], in_=ss[i][:], func=ACT.Relu, bias=-EPS * EPS)

        def rsqrt(i):
            if not inside(i, "fe"):
                return
            rinv[i] = small.tile([P, 2], F32, name="rinv", tag="rinv")
            nc.scalar.activation(out=rinv[i][:], in_=cl[i][:], func=ACT.Abs_reciprocal_sqrt, bias=EPS * EPS)

        def scale_out(i, j, on_vector):
            if not inside(i, "fe"):
                return
            if i not in o:
                o[i] = outs.tile([P, 2 * N], F32, name="o", tag="o")
            dst = o[i][:, j * N : (j + 1) * N]
            if on_vector:
                nc.vector.tensor_scalar(out=dst, in0=acc[(i, j)][:], scalar1=rinv[i][:, j : j + 1], scalar2=None, op0=ALU.mult)
            else:
                nc.scalar.activation(out=dst, in_=acc[(i, j)][:], func=ACT.Copy, scale=rinv[i][:, j : j + 1])

        def store(i, j0, j1):
            if not inside(i, "fe"):
                return
            kind, q = ORDER[i]
            view = o0_view if kind == "f" else o1_view
            c0 = q * 2 * N
            nc.sync.dma_start(out=view[:, c0 + j0 * N : c0 + j1 * N], in_=o[i][:, j0 * N : j1 * N])

        with tc.manual_schedule():
            idle_ps = psum_a.tile([P, N], F32, name="idle_ps", tag="acc")
            for i in range(WARM_FIRST):
                dummy()
            cast(0)
            for s in range(-6, LAST + 2, 2):
                quant(s + 2)
                quant(s + 3)
                if -4 < s <= 0:
                    cast(s + 4)
                for m in (s, s + 1):
                    sq(m, 0)
                    rsqrt(m - 1)
                    sq(m, 1)
                    over(m)
                    both_vector = not inside(m + 4, "e") and m - 1 != LAST
                    scale_out(m - 1, 0, True)
                    scale_out(m - 1, 1, both_vector)
                    mm(m + 2, 0)
                    mm(m + 2, 1)
                    copyout(m + 4)
                    trans(m + 6)
                    if m - 1 == LAST:
                        store(m - 1, 1, 2)
                        store(m - 1, 0, 1)
                    elif m - 1 >= LAST - FINE_STORES:
                        store(m - 1, 0, 1)
                        store(m - 1, 1, 2)
                    else:
                        store(m - 1, 0, 2)
